import numpy as np
import ml_dtypes


def mxq(x, axis, fmt="e4m3"):
    dtype, down = {"e4m3": (ml_dtypes.float8_e4m3fn, 7), "e5m2": (ml_dtypes.float8_e5m2, 14)}[fmt]
    v = np.moveaxis(np.asarray(x, np.float32).astype(ml_dtypes.bfloat16).astype(np.float64), axis, -1)
    blocks = v.reshape(v.shape[:-1] + (-1, 32))
    amax = np.abs(blocks).max(-1, keepdims=True)
    byte = np.maximum(np.where(amax > 0, np.frexp(amax)[1] - 1 + 127, 0) - down, 1)
    scale = np.exp2(byte - 127.0)
    codes = (blocks / scale).astype(np.float32).astype(dtype).astype(np.float64)
    return np.moveaxis((codes * scale).reshape(v.shape), -1, axis)


WIDE = False


def mx_kscale(k):
    if not WIDE:
        return np.ones(k)
    levels = np.array([10, -10, 5, -5, 0])
    if k % 512:
        return np.exp2(np.random.permutation(np.resize(levels, k // 32))).repeat(32)
    a = np.empty((k // 512, 16))
    for p in range(k // 512):
        a[p, :8] = np.random.permutation(np.resize(levels, 8))
        for g in range(8):
            far = levels[np.abs(levels - a[p, g]) >= 10]
            a[p, g + 8] = far[np.random.randint(len(far))]
    return np.exp2(a.ravel()).repeat(32)


BF16 = ml_dtypes.bfloat16


def bf(x):
    return np.asarray(x, np.float32).astype(BF16)


def f64(x):
    return np.asarray(x).astype(np.float64)


B, H, HKV, S, D = 1, 4, 2, 512, 128
G = H // HKV
NEG = -1e9


def setup_inputs():
    s = mx_kscale(S)
    keep = np.random.random((B, 1, S, S)) < 0.75
    return {"query": bf(np.random.standard_normal((B, H, S, D))),
            "key": bf(np.random.standard_normal((B, HKV, S, D))),
            "value": bf(np.random.standard_normal((B, HKV, S, D)) * 0.25 * np.sqrt(S) * s.max() / s[:, None]),
            "attention_mask": bf(np.where(keep, 0.5 * np.random.standard_normal((B, 1, S, S)) + np.log(s), NEG)),
            "sinks": bf(np.log(S * s.max()) - 3.5 + np.random.standard_normal(H))}


def reference(query, key, value, attention_mask, sinks):
    scaling = 1.0 / np.sqrt(D)
    k = np.repeat(f64(key), G, axis=1)
    attn = (f64(query) @ k.transpose(0, 1, 3, 2)) * scaling
    attn = attn + f64(attention_mask)[:, :, :, :attn.shape[-1]]
    sink_col = np.broadcast_to(f64(sinks).reshape(1, H, 1, 1), (B, H, S, 1))
    combined = np.concatenate([attn, sink_col], axis=-1)
    combined = combined - combined.max(-1, keepdims=True)
    e = np.exp(combined[..., :-1])
    den = e.sum(-1, keepdims=True) + np.exp(combined[..., -1:])
    eg = e.reshape(B, HKV, G * S, S)
    pv = mxq(eg, 3, "e4m3") @ mxq(f64(value), 2, "e4m3")
    out = pv.reshape(B, H, S, D) / den
    return out.transpose(0, 2, 1, 3)

@@ -1,0 +1,229 @@
+import math
+from contextlib import ExitStack
+
+import concourse.mybir as mybir
+from concourse.masks import make_identity
+
+BF16 = mybir.dt.bfloat16
+F32 = mybir.dt.float32
+U32 = mybir.dt.uint32
+U8 = mybir.dt.uint8
+FP8X4 = mybir.dt.float8_e4m3fn_x4
+ALU = mybir.AluOpType
+ACT = mybir.ActivationFunctionType
+
+P = 128
+PACK = 4
+PAIR = 2
+HALVES = PACK // PAIR
+HEADS = 4
+KV_HEADS = 2
+GROUP = HEADS // KV_HEADS
+SEQ = 512
+HEAD_DIM = 128
+Q_TILES = SEQ // P
+K_TILES = SEQ // P
+UNITS = Q_TILES * HEADS
+SCALING = 1.0 / math.sqrt(HEAD_DIM)
+
+FLOPS = 2 * 2 * HEADS * SEQ * SEQ * HEAD_DIM
+
+
+def tile_deepseekv4attention_s_kernel(tc, query, key, value, attention_mask, sinks, out):
+    nc = tc.nc
+
+    q_dram = [query[0, h].rearrange("(p r) d -> p r d", r=Q_TILES) for h in range(HEADS)]
+    mask_dram = attention_mask[0, 0].rearrange("(p r) k -> p r k", r=Q_TILES)
+    out_dram = out[0].rearrange("(p r) h d -> r h p d", r=Q_TILES)
+    k_dram = [key[0, g].rearrange("(t p u) d -> p t (u d)", p=P, u=HALVES) for g in range(KV_HEADS)]
+    v_dram = value[0].rearrange("g (p t) d -> p g (t d)", t=PACK)
+
+    with ExitStack() as ctx:
+        keep = ctx.enter_context(tc.tile_pool(name="keep", bufs=1))
+        work = ctx.enter_context(tc.tile_pool(name="work", bufs=3))
+        per_round = ctx.enter_context(tc.tile_pool(name="per_round", bufs=2))
+        results = ctx.enter_context(tc.tile_pool(name="results", bufs=6))
+        score_banks = ctx.enter_context(tc.psum_pool(name="score_banks", bufs=3))
+        flip_banks = ctx.enter_context(tc.psum_pool(name="flip_banks", bufs=2))
+        product_banks = ctx.enter_context(tc.psum_pool(name="product_banks", bufs=3))
+
+        sinks_bf = keep.tile([P, HEADS], BF16)
+        nc.scalar.dma_start(out=sinks_bf[:], in_=sinks.partition_broadcast(P))
+        k_sb = [keep.tile([P, K_TILES // HALVES, HALVES, HEAD_DIM], BF16, name="k_sb%d" % g) for g in range(KV_HEADS)]
+        q_sb = [keep.tile([P, Q_TILES, HEAD_DIM], BF16, name="q_sb%d" % h) for h in range(HEADS)]
+        mask_sb = keep.tile([P, Q_TILES, SEQ], BF16)
+        v_sb = keep.tile([P, KV_HEADS, PACK, HEAD_DIM], BF16)
+        nc.sync.dma_start(out=k_sb[0][:].rearrange("p t u d -> p t (u d)"), in_=k_dram[0])
+        nc.sync.dma_start(out=q_sb[0][:], in_=q_dram[0])
+        nc.sync.dma_start(out=v_sb[:].rearrange("p g t d -> p g (t d)"), in_=v_dram)
+        nc.sync.dma_start(out=mask_sb[:, 0:1, :], in_=mask_dram[:, 0:1, :])
+        nc.sync.dma_start(out=q_sb[1][:], in_=q_dram[1])
+        nc.sync.dma_start(out=k_sb[1][:].rearrange("p t u d -> p t (u d)"), in_=k_dram[1])
+        nc.sync.dma_start(out=q_sb[2][:], in_=q_dram[2])
+        nc.sync.dma_start(out=q_sb[3][:], in_=q_dram[3])
+        nc.sync.dma_start(out=mask_sb[:, 1:Q_TILES, :], in_=mask_dram[:, 1:Q_TILES, :])
+
+        identity_bf = keep.tile([P, P], BF16)
+        make_identity(nc, identity_bf[:])
+        identity_f32 = keep.tile([P, P], F32)
+        make_identity(nc, identity_f32[:])
+        zero = keep.tile([P, 1], F32)
+        one = keep.tile([P, 1], F32)
+        nc.vector.memset(zero[:], 0.0)
+        nc.scalar.activation(out=one[:], in_=zero[:], func=ACT.Exp)
+
+        s_sb = [keep.tile([P, SEQ + 1], F32, name="s_sb%d" % h) for h in range(HEADS)]
+
+        kT = [keep.tile([P, K_TILES, P], BF16, name="kT%d" % g) for g in range(KV_HEADS)]
+        qT = [keep.tile([P, Q_TILES, P], BF16, name="qT%d" % h) for h in range(HEADS)]
+        v_grouped = keep.tile([P, KV_HEADS, HEAD_DIM, PACK], BF16, align_bytes=64)
+        v_codes = keep.tile([P, KV_HEADS, HEAD_DIM], U32, align_bytes=64)
+        v_scales = keep.tile([P, KV_HEADS, HEAD_DIM], U8, align_bytes=64)
+
+        def transpose_rows(tiles, rowsT, copy):
+            flipped = flip_banks.tile([P, SEQ // P, P], BF16, tag="flipped")
+            for c in range(SEQ // P):
+                nc.tensor.transpose(flipped[:, c, :], tiles[c], identity_bf[:])
+            copy(out=rowsT[:], in_=flipped[:])
+
+        def k_tiles(g):
+            return [k_sb[g][:, t, u, :] for u in range(HALVES) for t in range(K_TILES // HALVES)]
+
+        def q_tiles(h):
+            return [q_sb[h][:, r, :] for r in range(Q_TILES)]
+
+        scores, neg_max, e_bf, e_flipped, e_grouped, e_codes, e_scales, product = (
+            {}, {}, {}, {}, {}, {}, {}, {},
+        )
+        den, inv_den = {}, {}
+
+        def multiply_qk(u):
+            r, h = divmod(u, HEADS)
+            scores[u] = score_banks.tile([P, SEQ], F32, name="scores")
+            nc.tensor.matmul(
+                out=scores[u][:],
+                lhsT=qT[h][:, r, :],
+                rhs=kT[h // GROUP][:].rearrange("d t p -> d (t p)"),
+                start=True,
+                stop=True,
+            )
+
+        def add_mask(u):
+            r, h = divmod(u, HEADS)
+            nc.vector.scalar_tensor_tensor(
+                out=s_sb[h][:, 0:SEQ].rearrange("p (u j) -> p u j", u=HALVES),
+                in0=scores[u][:].rearrange("p (u j) -> p u j", u=HALVES),
+                scalar=SCALING,
+                in1=mask_sb[:, r, :].rearrange("p (j u) -> p u j", u=HALVES),
+                op0=ALU.mult,
+                op1=ALU.add,
+            )
+
+        def negative_max(u):
+            h = u % HEADS
+            neg_max[u] = work.tile([P, 1], F32, name="neg_max")
+            nc.vector.tensor_reduce(
+                out=neg_max[u][:], in_=s_sb[h][:], axis=mybir.AxisListType.X, op=ALU.max, negate=True
+            )
+
+        def exponentials(u):
+            r, h = divmod(u, HEADS)
+            if h == 0:
+                den[r] = per_round.tile([P, HEADS], F32, name="den")
+            e_bf[u] = work.tile([P, SEQ + PAIR], BF16, name="e_bf")
+            nc.scalar.activation(
+                out=e_bf[u][:, 0 : SEQ + 1],
+                in_=s_sb[h][:],
+                func=ACT.Exp,
+                bias=neg_max[u][:],
+                scale=1.0,
+                accum_out=den[r][:, h : h + 1],
+            )
+
+        def transpose_e(u):
+            e_words = e_bf[u][:, 0:SEQ].bitcast(F32)
+            e_flipped[u] = flip_banks.tile([P, HALVES, P], F32, name="e_flipped", tag="flipped")
+            for j in range(HALVES):
+                nc.tensor.transpose(e_flipped[u][:, j, :], e_words[:, j * P : (j + 1) * P], identity_f32[:])
+
+        def group_e(u):
+            e_grouped[u] = work.tile([P, P, HALVES], F32, name="e_grouped", align_bytes=64)
+            nc.scalar.copy(out=e_grouped[u][:], in_=e_flipped[u][:].rearrange("p j q -> p q j"))
+
+        def quantise_e(u):
+            e_codes[u] = work.tile([P, P], U32, name="e_codes", align_bytes=64)
+            e_scales[u] = work.tile([P, P], U8, name="e_scales", align_bytes=64)
+            nc.vector.quantize_mx(
+                out=e_codes[u][:].bitcast(FP8X4),
+                scales=e_scales[u][:],
+                in_=e_grouped[u][:].rearrange("p q j -> p (q j)").bitcast(BF16),
+            )
+
+        def multiply_ev(u):
+            g = (u % HEADS) // GROUP
+            product[u] = product_banks.tile([P, HEAD_DIM], F32, name="product")
+            nc.tensor.matmul_mx(
+                out=product[u][:],
+                lhsT=e_codes[u][:].bitcast(FP8X4),
+                lhsT_scale=e_scales[u][:],
+                rhs=v_codes[:, g, :].bitcast(FP8X4),
+                rhs_scale=v_scales[:, g, :],
+                start=True,
+                stop=True,
+            )
+
+        def invert_den(r):
+            inv_den[r] = per_round.tile([P, HEADS], F32, name="inv_den")
+            nc.vector.reciprocal(out=inv_den[r][:], in_=den[r][:])
+
+        def divide_and_store(u):
+            r, h = divmod(u, HEADS)
+            result = results.tile([P, HEAD_DIM], F32)
+            nc.scalar.activation(
+                out=result[:], in_=product[u][:], func=ACT.Copy, scale=inv_den[r][:, h : h + 1]
+            )
+            nc.sync.dma_start(out=out_dram[r, h], in_=result[:])
+
+        transpose_rows(k_tiles(0), kT[0], nc.vector.tensor_copy)
+        transpose_rows(q_tiles(0), qT[0], nc.scalar.copy)
+        multiply_qk(0)
+        for g in range(KV_HEADS):
+            nc.vector.tensor_copy(
+                out=v_grouped[:, g].rearrange("p d (u e) -> p d u e", u=HALVES),
+                in_=v_sb[:, g].rearrange("p (e u) d -> p d u e", u=HALVES),
+            )
+        for h in range(HEADS):
+            nc.vector.tensor_copy(out=s_sb[h][:, SEQ : SEQ + 1], in_=sinks_bf[:, h : h + 1])
+        nc.vector.quantize_mx(
+            out=v_codes[:].rearrange("p g d -> p (g d)").bitcast(FP8X4),
+            scales=v_scales[:].rearrange("p g d -> p (g d)"),
+            in_=v_grouped[:].rearrange("p g d t -> p (g d t)"),
+        )
+        transpose_rows(q_tiles(1), qT[1], nc.scalar.copy)
+        multiply_qk(1)
+        add_mask(0)
+        transpose_rows(k_tiles(1), kT[1], nc.scalar.copy)
+        transpose_rows(q_tiles(2), qT[2], nc.scalar.copy)
+        transpose_rows(q_tiles(3), qT[3], nc.scalar.copy)
+
+        for n in range(UNITS + 7):
+            if n + 2 < UNITS:
+                multiply_qk(n + 2)
+            if 0 <= n - 2 < UNITS:
+                transpose_e(n - 2)
+            if 0 <= n - 4 < UNITS:
+                multiply_ev(n - 4)
+            if 0 <= n - 3 < UNITS:
+                group_e(n - 3)
+            if 0 <= n - 1 < UNITS:
+                exponentials(n - 1)
+            if 0 <= n - 6 < UNITS:
+                divide_and_store(n - 6)
+            if n + 1 < UNITS:
+                add_mask(n + 1)
+            if n < UNITS:
+                negative_max(n)
+            if 0 <= n - 3 < UNITS:
+                quantise_e(n - 3)
+            if n >= 5 and (n - 5) % HEADS == 0 and (n - 5) // HEADS < Q_TILES:
+                invert_den((n - 5) // HEADS)

@@ -23,8 +23,10 @@ SEQ = 512
 HEAD_DIM = 128
 Q_TILES = SEQ // P
 K_TILES = SEQ // P
-UNITS = Q_TILES * HEADS
+PAIRS = KV_HEADS * Q_TILES
+UNITS = PAIRS * GROUP
 SCALING = 1.0 / math.sqrt(HEAD_DIM)
+INV_SCALING = math.sqrt(HEAD_DIM)
 
 FLOPS = 2 * 2 * HEADS * SEQ * SEQ * HEAD_DIM
 
@@ -32,36 +34,49 @@ FLOPS = 2 * 2 * HEADS * SEQ * SEQ * HEAD_DIM
 def tile_deepseekv4attention_s_kernel(tc, query, key, value, attention_mask, sinks, out):
     nc = tc.nc
 
-    q_dram = [query[0, h].rearrange("(p r) d -> p r d", r=Q_TILES) for h in range(HEADS)]
+    q_dram = [
+        query[0, GROUP * g : GROUP * (g + 1)].rearrange("i (p r) d -> p i (r d)", r=Q_TILES) for g in range(KV_HEADS)
+    ]
     mask_dram = attention_mask[0, 0].rearrange("(p r) k -> p r k", r=Q_TILES)
-    out_dram = out[0].rearrange("(p r) h d -> r h p d", r=Q_TILES)
+    out_dram = out[0].rearrange("(p r) (g i) d -> r g p i d", r=Q_TILES, i=GROUP)
     k_dram = [key[0, g].rearrange("(t p u) d -> p t (u d)", p=P, u=HALVES) for g in range(KV_HEADS)]
     v_dram = value[0].rearrange("g (p t) d -> p g (t d)", t=PACK)
 
     with ExitStack() as ctx:
+        ctx.enter_context(tc.manual_schedule())
         keep = ctx.enter_context(tc.tile_pool(name="keep", bufs=1))
-        work = ctx.enter_context(tc.tile_pool(name="work", bufs=3))
-        per_round = ctx.enter_context(tc.tile_pool(name="per_round", bufs=2))
-        results = ctx.enter_context(tc.tile_pool(name="results", bufs=6))
-        score_banks = ctx.enter_context(tc.psum_pool(name="score_banks", bufs=3))
-        flip_banks = ctx.enter_context(tc.psum_pool(name="flip_banks", bufs=2))
-        product_banks = ctx.enter_context(tc.psum_pool(name="product_banks", bufs=3))
+        work = ctx.enter_context(tc.tile_pool(name="work", bufs=4))
+        small = ctx.enter_context(tc.tile_pool(name="small", bufs=4))
+        results = ctx.enter_context(tc.tile_pool(name="results", bufs=4))
+        score_banks = ctx.enter_context(tc.psum_pool(name="score_banks", bufs=4))
+        flip_banks = ctx.enter_context(tc.psum_pool(name="flip_banks", bufs=3))
+        product_banks = ctx.enter_context(tc.psum_pool(name="product_banks", bufs=1))
 
         sinks_bf = keep.tile([P, HEADS], BF16)
         nc.scalar.dma_start(out=sinks_bf[:], in_=sinks.partition_broadcast(P))
         k_sb = [keep.tile([P, K_TILES // HALVES, HALVES, HEAD_DIM], BF16, name="k_sb%d" % g) for g in range(KV_HEADS)]
-        q_sb = [keep.tile([P, Q_TILES, HEAD_DIM], BF16, name="q_sb%d" % h) for h in range(HEADS)]
-        mask_sb = keep.tile([P, Q_TILES, SEQ], BF16)
+        q_sb = [keep.tile([P, GROUP, Q_TILES, HEAD_DIM], BF16, name="q_sb%d" % g) for g in range(KV_HEADS)]
+        mask_sb = [keep.tile([P, SEQ], BF16, name="mask_sb%d" % r) for r in range(Q_TILES)]
         v_sb = keep.tile([P, KV_HEADS, PACK, HEAD_DIM], BF16)
-        nc.sync.dma_start(out=k_sb[0][:].rearrange("p t u d -> p t (u d)"), in_=k_dram[0])
-        nc.sync.dma_start(out=q_sb[0][:], in_=q_dram[0])
+
+        def load_k(g):
+            nc.sync.dma_start(out=k_sb[g][:].rearrange("p t u d -> p t (u d)"), in_=k_dram[g])
+
+        def load_q(g):
+            nc.sync.dma_start(out=q_sb[g][:].rearrange("p i r d -> p i (r d)"), in_=q_dram[g])
+
+        def load_mask(r):
+            nc.sync.dma_start(out=mask_sb[r][:], in_=mask_dram[:, r, :])
+
+        load_mask(0)
+        load_k(0)
+        load_q(0)
+        load_mask(1)
         nc.sync.dma_start(out=v_sb[:].rearrange("p g t d -> p g (t d)"), in_=v_dram)
-        nc.sync.dma_start(out=mask_sb[:, 0:1, :], in_=mask_dram[:, 0:1, :])
-        nc.sync.dma_start(out=q_sb[1][:], in_=q_dram[1])
-        nc.sync.dma_start(out=k_sb[1][:].rearrange("p t u d -> p t (u d)"), in_=k_dram[1])
-        nc.sync.dma_start(out=q_sb[2][:], in_=q_dram[2])
-        nc.sync.dma_start(out=q_sb[3][:], in_=q_dram[3])
-        nc.sync.dma_start(out=mask_sb[:, 1:Q_TILES, :], in_=mask_dram[:, 1:Q_TILES, :])
+        load_mask(2)
+        load_mask(3)
+        load_k(1)
+        load_q(1)
 
         identity_bf = keep.tile([P, P], BF16)
         make_identity(nc, identity_bf[:])
@@ -71,159 +86,233 @@ def tile_deepseekv4attention_s_kernel(tc, query, key, value, attention_mask, sin
         one = keep.tile([P, 1], F32)
         nc.vector.memset(zero[:], 0.0)
         nc.scalar.activation(out=one[:], in_=zero[:], func=ACT.Exp)
-
-        s_sb = [keep.tile([P, SEQ + 1], F32, name="s_sb%d" % h) for h in range(HEADS)]
+        neg_sinks = keep.tile([P, HEADS], F32)
+        nc.gpsimd.tensor_scalar(out=neg_sinks[:], in0=sinks_bf[:], scalar1=-1.0, scalar2=None, op0=ALU.mult)
 
         kT = [keep.tile([P, K_TILES, P], BF16, name="kT%d" % g) for g in range(KV_HEADS)]
-        qT = [keep.tile([P, Q_TILES, P], BF16, name="qT%d" % h) for h in range(HEADS)]
+        qT = [[keep.tile([P, GROUP, P], BF16, name="qT%d_%d" % (g, r)) for r in range(Q_TILES)] for g in range(KV_HEADS)]
+        maskT = [keep.tile([P, K_TILES, P], F32, name="maskT%d" % r) for r in range(Q_TILES)]
         v_grouped = keep.tile([P, KV_HEADS, HEAD_DIM, PACK], BF16, align_bytes=64)
         v_codes = keep.tile([P, KV_HEADS, HEAD_DIM], U32, align_bytes=64)
         v_scales = keep.tile([P, KV_HEADS, HEAD_DIM], U8, align_bytes=64)
 
-        def transpose_rows(tiles, rowsT, copy):
-            flipped = flip_banks.tile([P, SEQ // P, P], BF16, tag="flipped")
-            for c in range(SEQ // P):
-                nc.tensor.transpose(flipped[:, c, :], tiles[c], identity_bf[:])
-            copy(out=rowsT[:], in_=flipped[:])
+        def flip(tiles):
+            flipped = flip_banks.tile([P, len(tiles), P], BF16, name="flipped", tag="flipped")
+            for c, rows in enumerate(tiles):
+                nc.tensor.transpose(flipped[:, c, :], rows, identity_bf[:])
+            return flipped
 
-        def k_tiles(g):
-            return [k_sb[g][:, t, u, :] for u in range(HALVES) for t in range(K_TILES // HALVES)]
+        def flip_k(g):
+            return flip([k_sb[g][:, t, u, :] for u in range(HALVES) for t in range(K_TILES // HALVES)])
 
-        def q_tiles(h):
-            return [q_sb[h][:, r, :] for r in range(Q_TILES)]
+        def flip_q(g, rs):
+            return flip([q_sb[g][:, i, r, :] for r in rs for i in range(GROUP)])
 
-        scores, neg_max, e_bf, e_flipped, e_grouped, e_codes, e_scales, product = (
-            {}, {}, {}, {}, {}, {}, {}, {},
-        )
-        den, inv_den = {}, {}
+        def flip_mask(r):
+            halfway = SEQ // HALVES
+            return flip([
+                mask_sb[r][:, halfway * t + u : halfway * (t + 1) : HALVES]
+                for u in range(HALVES)
+                for t in range(K_TILES // HALVES)
+            ])
 
-        def multiply_qk(u):
-            r, h = divmod(u, HEADS)
-            scores[u] = score_banks.tile([P, SEQ], F32, name="scores")
-            nc.tensor.matmul(
-                out=scores[u][:],
-                lhsT=qT[h][:, r, :],
-                rhs=kT[h // GROUP][:].rearrange("d t p -> d (t p)"),
-                start=True,
-                stop=True,
-            )
+        def keep_q(g, rs, flipped, copy):
+            for k, r in enumerate(rs):
+                copy(out=qT[g][r][:], in_=flipped[:, GROUP * k : GROUP * (k + 1), :])
 
-        def add_mask(u):
-            r, h = divmod(u, HEADS)
-            nc.vector.scalar_tensor_tensor(
-                out=s_sb[h][:, 0:SEQ].rearrange("p (u j) -> p u j", u=HALVES),
-                in0=scores[u][:].rearrange("p (u j) -> p u j", u=HALVES),
-                scalar=SCALING,
-                in1=mask_sb[:, r, :].rearrange("p (j u) -> p u j", u=HALVES),
-                op0=ALU.mult,
-                op1=ALU.add,
-            )
+        def keep_mask(r, flipped):
+            nc.scalar.activation(out=maskT[r][:], in_=flipped[:], func=ACT.Copy, scale=INV_SCALING)
 
-        def negative_max(u):
-            h = u % HEADS
-            neg_max[u] = work.tile([P, 1], F32, name="neg_max")
-            nc.vector.tensor_reduce(
-                out=neg_max[u][:], in_=s_sb[h][:], axis=mybir.AxisListType.X, op=ALU.max, negate=True
-            )
-
-        def exponentials(u):
-            r, h = divmod(u, HEADS)
-            if h == 0:
-                den[r] = per_round.tile([P, HEADS], F32, name="den")
-            e_bf[u] = work.tile([P, SEQ + PAIR], BF16, name="e_bf")
-            nc.scalar.activation(
-                out=e_bf[u][:, 0 : SEQ + 1],
-                in_=s_sb[h][:],
-                func=ACT.Exp,
-                bias=neg_max[u][:],
-                scale=1.0,
-                accum_out=den[r][:, h : h + 1],
-            )
-
-        def transpose_e(u):
-            e_words = e_bf[u][:, 0:SEQ].bitcast(F32)
-            e_flipped[u] = flip_banks.tile([P, HALVES, P], F32, name="e_flipped", tag="flipped")
-            for j in range(HALVES):
-                nc.tensor.transpose(e_flipped[u][:, j, :], e_words[:, j * P : (j + 1) * P], identity_f32[:])
-
-        def group_e(u):
-            e_grouped[u] = work.tile([P, P, HALVES], F32, name="e_grouped", align_bytes=64)
-            nc.scalar.copy(out=e_grouped[u][:], in_=e_flipped[u][:].rearrange("p j q -> p q j"))
-
-        def quantise_e(u):
-            e_codes[u] = work.tile([P, P], U32, name="e_codes", align_bytes=64)
-            e_scales[u] = work.tile([P, P], U8, name="e_scales", align_bytes=64)
-            nc.vector.quantize_mx(
-                out=e_codes[u][:].bitcast(FP8X4),
-                scales=e_scales[u][:],
-                in_=e_grouped[u][:].rearrange("p q j -> p (q j)").bitcast(BF16),
-            )
-
-        def multiply_ev(u):
-            g = (u % HEADS) // GROUP
-            product[u] = product_banks.tile([P, HEAD_DIM], F32, name="product")
-            nc.tensor.matmul_mx(
-                out=product[u][:],
-                lhsT=e_codes[u][:].bitcast(FP8X4),
-                lhsT_scale=e_scales[u][:],
-                rhs=v_codes[:, g, :].bitcast(FP8X4),
-                rhs_scale=v_scales[:, g, :],
-                start=True,
-                stop=True,
-            )
-
-        def invert_den(r):
-            inv_den[r] = per_round.tile([P, HEADS], F32, name="inv_den")
-            nc.vector.reciprocal(out=inv_den[r][:], in_=den[r][:])
-
-        def divide_and_store(u):
-            r, h = divmod(u, HEADS)
-            result = results.tile([P, HEAD_DIM], F32)
-            nc.scalar.activation(
-                out=result[:], in_=product[u][:], func=ACT.Copy, scale=inv_den[r][:, h : h + 1]
-            )
-            nc.sync.dma_start(out=out_dram[r, h], in_=result[:])
-
-        transpose_rows(k_tiles(0), kT[0], nc.vector.tensor_copy)
-        transpose_rows(q_tiles(0), qT[0], nc.scalar.copy)
-        multiply_qk(0)
-        for g in range(KV_HEADS):
+        def group_value(g):
             nc.vector.tensor_copy(
                 out=v_grouped[:, g].rearrange("p d (u e) -> p d u e", u=HALVES),
                 in_=v_sb[:, g].rearrange("p (e u) d -> p d u e", u=HALVES),
             )
-        for h in range(HEADS):
-            nc.vector.tensor_copy(out=s_sb[h][:, SEQ : SEQ + 1], in_=sinks_bf[:, h : h + 1])
-        nc.vector.quantize_mx(
-            out=v_codes[:].rearrange("p g d -> p (g d)").bitcast(FP8X4),
-            scales=v_scales[:].rearrange("p g d -> p (g d)"),
-            in_=v_grouped[:].rearrange("p g d t -> p (g d t)"),
-        )
-        transpose_rows(q_tiles(1), qT[1], nc.scalar.copy)
-        multiply_qk(1)
-        add_mask(0)
-        transpose_rows(k_tiles(1), kT[1], nc.scalar.copy)
-        transpose_rows(q_tiles(2), qT[2], nc.scalar.copy)
-        transpose_rows(q_tiles(3), qT[3], nc.scalar.copy)
 
-        for n in range(UNITS + 7):
-            if n + 2 < UNITS:
-                multiply_qk(n + 2)
-            if 0 <= n - 2 < UNITS:
-                transpose_e(n - 2)
-            if 0 <= n - 4 < UNITS:
-                multiply_ev(n - 4)
-            if 0 <= n - 3 < UNITS:
-                group_e(n - 3)
-            if 0 <= n - 1 < UNITS:
-                exponentials(n - 1)
-            if 0 <= n - 6 < UNITS:
-                divide_and_store(n - 6)
-            if n + 1 < UNITS:
-                add_mask(n + 1)
-            if n < UNITS:
-                negative_max(n)
-            if 0 <= n - 3 < UNITS:
-                quantise_e(n - 3)
-            if n >= 5 and (n - 5) % HEADS == 0 and (n - 5) // HEADS < Q_TILES:
-                invert_den((n - 5) // HEADS)
+        def quantise_value():
+            nc.vector.quantize_mx(
+                out=v_codes[:].rearrange("p g d -> p (g d)").bitcast(FP8X4),
+                scales=v_scales[:].rearrange("p g d -> p (g d)"),
+                in_=v_grouped[:].rearrange("p g d t -> p (g d t)"),
+            )
+
+        scores, e_bf, e_flipped, e_grouped, e_codes, e_scales = ({}, {}, {}, {}, {}, {})
+        neg_x, neg_max, row_sum, sink_arg, sink_e, den, inv_den, product = ({}, {}, {}, {}, {}, {}, {}, {})
+
+        def multiply_qk(j):
+            n, i = divmod(j, GROUP)
+            g, r = divmod(n, Q_TILES)
+            scores[j] = score_banks.tile([P, SEQ], F32, name="scores")
+            for c in range(K_TILES):
+                nc.tensor.matmul(
+                    out=scores[j][:, c * P : (c + 1) * P],
+                    lhsT=maskT[r][:, c, :],
+                    rhs=identity_f32[:],
+                    start=(c == 0),
+                    stop=False,
+                    is_transpose=True,
+                )
+            nc.tensor.matmul(
+                out=scores[j][:],
+                lhsT=qT[g][r][:, i, :],
+                rhs=kT[g][:].rearrange("d t p -> d (t p)"),
+                start=False,
+                stop=True,
+            )
+
+        def row_max(j):
+            n, i = divmod(j, GROUP)
+            if i == 0:
+                neg_x[n] = small.tile([P, GROUP], F32, name="neg_x")
+            nc.vector.tensor_reduce(
+                out=neg_x[n][:, i : i + 1], in_=scores[j][:], axis=mybir.AxisListType.X, op=ALU.max, negate=True
+            )
+
+        def negative_max(n, first=0, last=GROUP):
+            g = n // Q_TILES
+            if first == 0:
+                neg_max[n] = small.tile([P, GROUP], F32, name="neg_max")
+            nc.vector.scalar_tensor_tensor(
+                out=neg_max[n][:, first:last],
+                in0=neg_x[n][:, first:last],
+                scalar=SCALING,
+                in1=neg_sinks[:, GROUP * g + first : GROUP * g + last],
+                op0=ALU.mult,
+                op1=ALU.min,
+            )
+            if last == GROUP:
+                sink_arg[n] = small.tile([P, GROUP], F32, name="sink_arg")
+                nc.gpsimd.tensor_sub(sink_arg[n][:], neg_max[n][:], neg_sinks[:, GROUP * g : GROUP * (g + 1)])
+
+        def exponentials(j):
+            n, i = divmod(j, GROUP)
+            if i == 0:
+                row_sum[n] = small.tile([P, GROUP], F32, name="row_sum")
+            e_bf[j] = work.tile([P, SEQ], BF16, name="e_bf")
+            nc.scalar.activation(
+                out=e_bf[j][:],
+                in_=scores[j][:],
+                func=ACT.Exp,
+                bias=neg_max[n][:, i : i + 1],
+                scale=SCALING,
+                accum_out=row_sum[n][:, i : i + 1],
+            )
+
+        def denominator(n):
+            sink_e[n] = small.tile([P, GROUP], F32, name="sink_e")
+            nc.scalar.activation(out=sink_e[n][:], in_=sink_arg[n][:], func=ACT.Exp)
+            den[n] = small.tile([P, GROUP], F32, name="den")
+            nc.gpsimd.tensor_add(den[n][:], row_sum[n][:], sink_e[n][:])
+
+        def transpose_e(j):
+            e_words = e_bf[j][:].bitcast(F32)
+            e_flipped[j] = flip_banks.tile([P, HALVES, P], F32, name="e_flipped", tag="flipped")
+            for u in range(HALVES):
+                nc.tensor.transpose(e_flipped[j][:, u, :], e_words[:, u * P : (u + 1) * P], identity_f32[:])
+
+        def group_e(j):
+            e_grouped[j] = work.tile([P, P, HALVES], F32, name="e_grouped", align_bytes=64)
+            nc.scalar.copy(out=e_grouped[j][:], in_=e_flipped[j][:].rearrange("p u q -> p q u"))
+
+        def quantise_e(j):
+            e_codes[j] = work.tile([P, P], U32, name="e_codes", align_bytes=64)
+            e_scales[j] = work.tile([P, P], U8, name="e_scales", align_bytes=64)
+            nc.vector.quantize_mx(
+                out=e_codes[j][:].bitcast(FP8X4),
+                scales=e_scales[j][:],
+                in_=e_grouped[j][:].rearrange("p q u -> p (q u)").bitcast(BF16),
+            )
+
+        def multiply_ev(n):
+            g = n // Q_TILES
+            product[n] = product_banks.tile([P, GROUP, HEAD_DIM], F32, name="product")
+            for i in range(GROUP):
+                nc.tensor.matmul_mx(
+                    out=product[n][:, i, :],
+                    lhsT=e_codes[GROUP * n + i][:].bitcast(FP8X4),
+                    lhsT_scale=e_scales[GROUP * n + i][:],
+                    rhs=v_codes[:, g, :].bitcast(FP8X4),
+                    rhs_scale=v_scales[:, g, :],
+                    start=True,
+                    stop=True,
+                )
+
+        def invert_den(n):
+            inv_den[n] = small.tile([P, GROUP], F32, name="inv_den")
+            nc.vector.reciprocal(out=inv_den[n][:], in_=den[n][:])
+
+        def divide_and_store(n):
+            g, r = divmod(n, Q_TILES)
+            result = results.tile([P, GROUP, HEAD_DIM], F32)
+            nc.vector.tensor_tensor(
+                out=result[:],
+                in0=product[n][:],
+                in1=inv_den[n][:].unsqueeze(2).to_broadcast([P, GROUP, HEAD_DIM]),
+                op=ALU.mult,
+            )
+            nc.sync.dma_start(out=out_dram[r, g], in_=result[:])
+
+        flipped_m = flip_mask(0)
+        flipped_k = flip_k(0)
+        keep_mask(0, flipped_m)
+        nc.vector.tensor_copy(out=kT[0][:], in_=flipped_k[:])
+        flipped_q = flip_q(0, [0])
+        keep_q(0, [0], flipped_q, nc.scalar.copy)
+        flipped_m = flip_mask(1)
+        multiply_qk(0)
+        keep_mask(1, flipped_m)
+        multiply_qk(1)
+        flipped_q = flip_q(0, [1])
+        flipped_m = flip_mask(2)
+        keep_q(0, [1], flipped_q, nc.scalar.copy)
+        keep_mask(2, flipped_m)
+        multiply_qk(2)
+        group_value(0)
+        row_max(0)
+        group_value(1)
+        negative_max(0, 0, 1)
+        row_max(1)
+        quantise_value()
+        negative_max(0, 1, GROUP)
+        flipped_q = flip_q(0, [2, 3])
+
+        for j in range(UNITS + 6):
+            n, i = divmod(j, GROUP)
+            if 0 <= j - 1 < UNITS:
+                transpose_e(j - 1)
+            if j + 3 < UNITS:
+                multiply_qk(j + 3)
+            if i == 0 and 0 <= n - 2 < PAIRS:
+                multiply_ev(n - 2)
+            if j < UNITS:
+                exponentials(j)
+            if 0 <= j - 1 < UNITS:
+                group_e(j - 1)
+            if i == 1 and n < PAIRS:
+                denominator(n)
+            if j == 2:
+                keep_mask(3, flipped_m)
+            if j + 2 < UNITS:
+                row_max(j + 2)
+            if 0 <= j - 2 < UNITS:
+                quantise_e(j - 2)
+            if j == 0:
+                keep_q(0, [2, 3], flipped_q, nc.vector.tensor_copy)
+                flipped_m = flip_mask(3)
+            if j == 2:
+                flipped_k = flip_k(1)
+            if j == 3:
+                nc.vector.tensor_copy(out=kT[1][:], in_=flipped_k[:])
+                flipped_q = flip_q(1, [0, 1])
+            if j == 4:
+                keep_q(1, [0, 1], flipped_q, nc.vector.tensor_copy)
+            if j == 5:
+                flipped_q = flip_q(1, [2, 3])
+            if j == 6:
+                keep_q(1, [2, 3], flipped_q, nc.vector.tensor_copy)
+            if i == 1 and n + 1 < PAIRS:
+                negative_max(n + 1)
+            if i == 0 and 0 <= n - 2 < PAIRS:
+                invert_den(n - 2)
+            if i == 1 and 0 <= n - 2 < PAIRS:
+                divide_and_store(n - 2)

@@ -27,6 +27,8 @@ PAIRS = KV_HEADS * Q_TILES
 UNITS = PAIRS * GROUP
 SCALING = 1.0 / math.sqrt(HEAD_DIM)
 INV_SCALING = math.sqrt(HEAD_DIM)
+PAIR_ORDER = [(0, r) for r in range(Q_TILES)] + [(1, (r + 1) % Q_TILES) for r in range(Q_TILES)]
+VECTOR_PAIRS = 1
 
 FLOPS = 2 * 2 * HEADS * SEQ * SEQ * HEAD_DIM
 
@@ -35,7 +37,7 @@ def tile_deepseekv4attention_s_kernel(tc, query, key, value, attention_mask, sin
     nc = tc.nc
 
     q_dram = [
-        query[0, GROUP * g : GROUP * (g + 1)].rearrange("i (p r) d -> p i (r d)", r=Q_TILES) for g in range(KV_HEADS)
+        query[0, GROUP * g : GROUP * (g + 1)].rearrange("i (p r) d -> p i r d", r=Q_TILES) for g in range(KV_HEADS)
     ]
     mask_dram = attention_mask[0, 0].rearrange("(p r) k -> p r k", r=Q_TILES)
     out_dram = out[0].rearrange("(p r) (g i) d -> r g p i d", r=Q_TILES, i=GROUP)
@@ -55,28 +57,32 @@ def tile_deepseekv4attention_s_kernel(tc, query, key, value, attention_mask, sin
         sinks_bf = keep.tile([P, HEADS], BF16)
         nc.scalar.dma_start(out=sinks_bf[:], in_=sinks.partition_broadcast(P))
         k_sb = [keep.tile([P, K_TILES // HALVES, HALVES, HEAD_DIM], BF16, name="k_sb%d" % g) for g in range(KV_HEADS)]
-        q_sb = [keep.tile([P, GROUP, Q_TILES, HEAD_DIM], BF16, name="q_sb%d" % g) for g in range(KV_HEADS)]
+        q_sb = {}
         mask_sb = [keep.tile([P, SEQ], BF16, name="mask_sb%d" % r) for r in range(Q_TILES)]
         v_sb = keep.tile([P, KV_HEADS, PACK, HEAD_DIM], BF16)
 
         def load_k(g):
             nc.sync.dma_start(out=k_sb[g][:].rearrange("p t u d -> p t (u d)"), in_=k_dram[g])
 
-        def load_q(g):
-            nc.sync.dma_start(out=q_sb[g][:].rearrange("p i r d -> p i (r d)"), in_=q_dram[g])
+        def load_q(g, first, last):
+            rows = keep.tile([P, GROUP, last - first, HEAD_DIM], BF16, name="q_sb%d_%d" % (g, first))
+            nc.sync.dma_start(out=rows[:], in_=q_dram[g][:, :, first:last, :])
+            for r in range(first, last):
+                q_sb[g, r] = rows[:, :, r - first, :]
 
         def load_mask(r):
             nc.sync.dma_start(out=mask_sb[r][:], in_=mask_dram[:, r, :])
 
-        load_mask(0)
         load_k(0)
-        load_q(0)
+        load_q(0, 0, 1)
+        load_mask(0)
         load_mask(1)
-        nc.sync.dma_start(out=v_sb[:].rearrange("p g t d -> p g (t d)"), in_=v_dram)
+        load_q(0, 1, Q_TILES)
         load_mask(2)
+        nc.sync.dma_start(out=v_sb[:].rearrange("p g t d -> p g (t d)"), in_=v_dram)
         load_mask(3)
         load_k(1)
-        load_q(1)
+        load_q(1, 0, Q_TILES)
 
         identity_bf = keep.tile([P, P], BF16)
         make_identity(nc, identity_bf[:])
@@ -106,7 +112,7 @@ def tile_deepseekv4attention_s_kernel(tc, query, key, value, attention_mask, sin
             return flip([k_sb[g][:, t, u, :] for u in range(HALVES) for t in range(K_TILES // HALVES)])
 
         def flip_q(g, rs):
-            return flip([q_sb[g][:, i, r, :] for r in rs for i in range(GROUP)])
+            return flip([q_sb[g, r][:, i, :] for r in rs for i in range(GROUP)])
 
         def flip_mask(r):
             halfway = SEQ // HALVES
@@ -141,24 +147,42 @@ def tile_deepseekv4attention_s_kernel(tc, query, key, value, attention_mask, sin
 
         def multiply_qk(j):
             n, i = divmod(j, GROUP)
-            g, r = divmod(n, Q_TILES)
+            g, r = PAIR_ORDER[n]
             scores[j] = score_banks.tile([P, SEQ], F32, name="scores")
-            for c in range(K_TILES):
-                nc.tensor.matmul(
-                    out=scores[j][:, c * P : (c + 1) * P],
-                    lhsT=maskT[r][:, c, :],
-                    rhs=identity_f32[:],
-                    start=(c == 0),
-                    stop=False,
-                    is_transpose=True,
-                )
+            on_tensor = n >= VECTOR_PAIRS
+            if on_tensor:
+                for c in range(K_TILES):
+                    nc.tensor.matmul(
+                        out=scores[j][:, c * P : (c + 1) * P],
+                        lhsT=maskT[r][:, c, :],
+                        rhs=identity_f32[:],
+                        start=(c == 0),
+                        stop=False,
+                        is_transpose=True,
+                    )
             nc.tensor.matmul(
                 out=scores[j][:],
                 lhsT=qT[g][r][:, i, :],
                 rhs=kT[g][:].rearrange("d t p -> d (t p)"),
-                start=False,
+                start=not on_tensor,
                 stop=True,
             )
+
+        def add_mask(j):
+            n = j // GROUP
+            if n >= VECTOR_PAIRS:
+                return
+            r = PAIR_ORDER[n][1]
+            masked = work.tile([P, SEQ], F32, name="masked")
+            nc.vector.scalar_tensor_tensor(
+                out=masked[:].rearrange("p (u j) -> p u j", u=HALVES),
+                in0=mask_sb[r][:].rearrange("p (j u) -> p u j", u=HALVES),
+                scalar=INV_SCALING,
+                in1=scores[j][:].rearrange("p (u j) -> p u j", u=HALVES),
+                op0=ALU.mult,
+                op1=ALU.add,
+            )
+            scores[j] = masked
 
         def row_max(j):
             n, i = divmod(j, GROUP)
@@ -169,7 +193,7 @@ def tile_deepseekv4attention_s_kernel(tc, query, key, value, attention_mask, sin
             )
 
         def negative_max(n, first=0, last=GROUP):
-            g = n // Q_TILES
+            g = PAIR_ORDER[n][0]
             if first == 0:
                 neg_max[n] = small.tile([P, GROUP], F32, name="neg_max")
             nc.vector.scalar_tensor_tensor(
@@ -224,7 +248,7 @@ def tile_deepseekv4attention_s_kernel(tc, query, key, value, attention_mask, sin
             )
 
         def multiply_ev(n):
-            g = n // Q_TILES
+            g = PAIR_ORDER[n][0]
             product[n] = product_banks.tile([P, GROUP, HEAD_DIM], F32, name="product")
             for i in range(GROUP):
                 nc.tensor.matmul_mx(
@@ -242,7 +266,7 @@ def tile_deepseekv4attention_s_kernel(tc, query, key, value, attention_mask, sin
             nc.vector.reciprocal(out=inv_den[n][:], in_=den[n][:])
 
         def divide_and_store(n):
-            g, r = divmod(n, Q_TILES)
+            g, r = PAIR_ORDER[n]
             result = results.tile([P, GROUP, HEAD_DIM], F32)
             nc.vector.tensor_tensor(
                 out=result[:],
@@ -252,29 +276,28 @@ def tile_deepseekv4attention_s_kernel(tc, query, key, value, attention_mask, sin
             )
             nc.sync.dma_start(out=out_dram[r, g], in_=result[:])
 
-        flipped_m = flip_mask(0)
         flipped_k = flip_k(0)
-        keep_mask(0, flipped_m)
         nc.vector.tensor_copy(out=kT[0][:], in_=flipped_k[:])
         flipped_q = flip_q(0, [0])
         keep_q(0, [0], flipped_q, nc.scalar.copy)
-        flipped_m = flip_mask(1)
         multiply_qk(0)
+        flipped_m = flip_mask(1)
         keep_mask(1, flipped_m)
         multiply_qk(1)
         flipped_q = flip_q(0, [1])
-        flipped_m = flip_mask(2)
         keep_q(0, [1], flipped_q, nc.scalar.copy)
+        flipped_m = flip_mask(2)
         keep_mask(2, flipped_m)
         multiply_qk(2)
+        add_mask(0)
         group_value(0)
         row_max(0)
-        group_value(1)
+        add_mask(1)
         negative_max(0, 0, 1)
         row_max(1)
-        quantise_value()
-        negative_max(0, 1, GROUP)
         flipped_q = flip_q(0, [2, 3])
+        group_value(1)
+        negative_max(0, 1, GROUP)
 
         for j in range(UNITS + 6):
             n, i = divmod(j, GROUP)
@@ -284,32 +307,40 @@ def tile_deepseekv4attention_s_kernel(tc, query, key, value, attention_mask, sin
                 multiply_qk(j + 3)
             if i == 0 and 0 <= n - 2 < PAIRS:
                 multiply_ev(n - 2)
+            if j == 0:
+                flipped_m = flip_mask(3)
+            if j == 1:
+                flipped_k = flip_k(1)
+            if j == 3:
+                flipped_q = flip_q(1, [0, 1])
+            if j == 5:
+                flipped_q = flip_q(1, [2, 3])
+            if j == 7:
+                flipped_m = flip_mask(0)
             if j < UNITS:
                 exponentials(j)
+            if j == 0:
+                keep_q(0, [2, 3], flipped_q, nc.scalar.copy)
+            if j == 1:
+                keep_mask(3, flipped_m)
             if 0 <= j - 1 < UNITS:
                 group_e(j - 1)
             if i == 1 and n < PAIRS:
                 denominator(n)
-            if j == 2:
-                keep_mask(3, flipped_m)
             if j + 2 < UNITS:
                 row_max(j + 2)
+            if j == 1:
+                quantise_value()
             if 0 <= j - 2 < UNITS:
                 quantise_e(j - 2)
-            if j == 0:
-                keep_q(0, [2, 3], flipped_q, nc.vector.tensor_copy)
-                flipped_m = flip_mask(3)
             if j == 2:
-                flipped_k = flip_k(1)
-            if j == 3:
                 nc.vector.tensor_copy(out=kT[1][:], in_=flipped_k[:])
-                flipped_q = flip_q(1, [0, 1])
             if j == 4:
                 keep_q(1, [0, 1], flipped_q, nc.vector.tensor_copy)
-            if j == 5:
-                flipped_q = flip_q(1, [2, 3])
             if j == 6:
                 keep_q(1, [2, 3], flipped_q, nc.vector.tensor_copy)
+            if j == 8:
+                keep_mask(0, flipped_m)
             if i == 1 and n + 1 < PAIRS:
                 negative_max(n + 1)
             if i == 0 and 0 <= n - 2 < PAIRS:

@@ -54,8 +54,11 @@ def tile_deepseekv4attention_s_kernel(tc, query, key, value, attention_mask, sin
         flip_banks = ctx.enter_context(tc.psum_pool(name="flip_banks", bufs=3))
         product_banks = ctx.enter_context(tc.psum_pool(name="product_banks", bufs=1))
 
-        sinks_bf = keep.tile([P, HEADS], BF16)
-        nc.scalar.dma_start(out=sinks_bf[:], in_=sinks.partition_broadcast(P))
+        sinks_row = keep.tile([P, HEADS], BF16)
+        ones_bf = keep.tile([P, P], BF16)
+        nc.vector.memset(sinks_row[:], 0.0)
+        nc.vector.memset(ones_bf[:], 1.0)
+        nc.scalar.dma_start(out=sinks_row[0:1, :], in_=sinks.unsqueeze(0))
         k_sb = [keep.tile([P, K_TILES // HALVES, HALVES, HEAD_DIM], BF16, name="k_sb%d" % g) for g in range(KV_HEADS)]
         q_sb = {}
         mask_sb = [keep.tile([P, SEQ], BF16, name="mask_sb%d" % r) for r in range(Q_TILES)]
@@ -93,7 +96,6 @@ def tile_deepseekv4attention_s_kernel(tc, query, key, value, attention_mask, sin
         nc.vector.memset(zero[:], 0.0)
         nc.scalar.activation(out=one[:], in_=zero[:], func=ACT.Exp)
         neg_sinks = keep.tile([P, HEADS], F32)
-        nc.gpsimd.tensor_scalar(out=neg_sinks[:], in0=sinks_bf[:], scalar1=-1.0, scalar2=None, op0=ALU.mult)
 
         kT = [keep.tile([P, K_TILES, P], BF16, name="kT%d" % g) for g in range(KV_HEADS)]
         qT = [[keep.tile([P, GROUP, P], BF16, name="qT%d_%d" % (g, r)) for r in range(Q_TILES)] for g in range(KV_HEADS)]
@@ -249,7 +251,7 @@ def tile_deepseekv4attention_s_kernel(tc, query, key, value, attention_mask, sin
 
         def multiply_ev(n):
             g = PAIR_ORDER[n][0]
-            product[n] = product_banks.tile([P, GROUP, HEAD_DIM], F32, name="product")
+            product[n] = product_banks.tile([P, GROUP, HEAD_DIM], F32, name="product", tag="product")
             for i in range(GROUP):
                 nc.tensor.matmul_mx(
                     out=product[n][:, i, :],
@@ -284,6 +286,8 @@ def tile_deepseekv4attention_s_kernel(tc, query, key, value, attention_mask, sin
         flipped_m = flip_mask(1)
         keep_mask(1, flipped_m)
         multiply_qk(1)
+        spread_sinks = product_banks.tile([P, HEADS], F32, name="spread_sinks", tag="product")
+        nc.tensor.matmul(out=spread_sinks[:], lhsT=ones_bf[:], rhs=sinks_row[:], start=True, stop=True)
         flipped_q = flip_q(0, [1])
         keep_q(0, [1], flipped_q, nc.scalar.copy)
         flipped_m = flip_mask(2)
@@ -292,6 +296,7 @@ def tile_deepseekv4attention_s_kernel(tc, query, key, value, attention_mask, sin
         add_mask(0)
         group_value(0)
         row_max(0)
+        nc.vector.tensor_scalar_mul(neg_sinks[:], spread_sinks[:], -1.0)
         add_mask(1)
         negative_max(0, 0, 1)
         row_max(1)

@@ -150,7 +150,7 @@ def tile_deepseekv4attention_s_kernel(tc, query, key, value, attention_mask, sin
         def multiply_qk(j):
             n, i = divmod(j, GROUP)
             g, r = PAIR_ORDER[n]
-            scores[j] = score_banks.tile([P, SEQ], F32, name="scores")
+            scores[j] = score_banks.tile([P, SEQ], F32, name="scores", tag="scores")
             on_tensor = n >= VECTOR_PAIRS
             if on_tensor:
                 for c in range(K_TILES):
@@ -249,16 +249,36 @@ def tile_deepseekv4attention_s_kernel(tc, query, key, value, attention_mask, sin
                 in_=e_grouped[j][:].rearrange("p q u -> p (q u)").bitcast(BF16),
             )
 
-        def multiply_ev(n):
-            g = PAIR_ORDER[n][0]
+        def multiply_ev(j, out):
+            g = PAIR_ORDER[j // GROUP][0]
+            nc.tensor.matmul_mx(
+                out=out,
+                lhsT=e_codes[j][:].bitcast(FP8X4),
+                lhsT_scale=e_scales[j][:],
+                rhs=v_codes[:, g, :].bitcast(FP8X4),
+                rhs_scale=v_scales[:, g, :],
+                start=True,
+                stop=True,
+            )
+
+        def multiply_ev_pair(n):
             product[n] = product_banks.tile([P, GROUP, HEAD_DIM], F32, name="product", tag="product")
             for i in range(GROUP):
+                multiply_ev(GROUP * n + i, product[n][:, i, :])
+
+        def multiply_ev_unit(j):
+            product[j] = score_banks.tile([P, HEAD_DIM], F32, name="product_unit", tag="scores")
+            multiply_ev(j, product[j][:])
+
+        def keep_warm():
+            idle = score_banks.tile([P, KV_HEADS * HEAD_DIM], F32, name="idle", tag="scores")
+            for k in range(2):
                 nc.tensor.matmul_mx(
-                    out=product[n][:, i, :],
-                    lhsT=e_codes[GROUP * n + i][:].bitcast(FP8X4),
-                    lhsT_scale=e_scales[GROUP * n + i][:],
-                    rhs=v_codes[:, g, :].bitcast(FP8X4),
-                    rhs_scale=v_scales[:, g, :],
+                    out=idle[:],
+                    lhsT=v_codes[:, 0, :].bitcast(FP8X4),
+                    lhsT_scale=v_scales[:, 0, :],
+                    rhs=v_codes[:].rearrange("p g d -> p (g d)").bitcast(FP8X4),
+                    rhs_scale=v_scales[:].rearrange("p g d -> p (g d)"),
                     start=True,
                     stop=True,
                 )
@@ -277,6 +297,13 @@ def tile_deepseekv4attention_s_kernel(tc, query, key, value, attention_mask, sin
                 op=ALU.mult,
             )
             nc.sync.dma_start(out=out_dram[r, g], in_=result[:])
+
+        def divide_and_store_unit(j):
+            n, i = divmod(j, GROUP)
+            g, r = PAIR_ORDER[n]
+            result = results.tile([P, HEAD_DIM], F32, name="result_unit")
+            nc.vector.tensor_scalar_mul(result[:], product[j][:], inv_den[n][:, i : i + 1])
+            nc.sync.dma_start(out=out_dram[r, g][:, i, :], in_=result[:])
 
         flipped_k = flip_k(0)
         nc.vector.tensor_copy(out=kT[0][:], in_=flipped_k[:])
@@ -304,14 +331,19 @@ def tile_deepseekv4attention_s_kernel(tc, query, key, value, attention_mask, sin
         group_value(1)
         negative_max(0, 1, GROUP)
 
-        for j in range(UNITS + 6):
+        LAST = UNITS - GROUP
+        for j in range(UNITS + 3):
             n, i = divmod(j, GROUP)
             if 0 <= j - 1 < UNITS:
                 transpose_e(j - 1)
             if j + 3 < UNITS:
                 multiply_qk(j + 3)
-            if i == 0 and 0 <= n - 2 < PAIRS:
-                multiply_ev(n - 2)
+            if i == 0 and 0 <= n - 2 < PAIRS - 1:
+                multiply_ev_pair(n - 2)
+            if 0 <= j - 3 - LAST < GROUP:
+                multiply_ev_unit(j - 3)
+            if j in (LAST - 1, LAST, UNITS):
+                keep_warm()
             if j == 0:
                 flipped_m = flip_mask(3)
             if j == 1:
@@ -348,7 +380,11 @@ def tile_deepseekv4attention_s_kernel(tc, query, key, value, attention_mask, sin
                 keep_mask(0, flipped_m)
             if i == 1 and n + 1 < PAIRS:
                 negative_max(n + 1)
-            if i == 0 and 0 <= n - 2 < PAIRS:
+            if i == 0 and 0 <= n - 2 < PAIRS - 1:
                 invert_den(n - 2)
-            if i == 1 and 0 <= n - 2 < PAIRS:
+            if i == 1 and 0 <= n - 2 < PAIRS - 1:
                 divide_and_store(n - 2)
+            if j == LAST + 3:
+                invert_den(PAIRS - 1)
+            if 0 <= j - 3 - LAST < GROUP:
+                divide_and_store_unit(j - 3)

@@ -50,9 +50,8 @@ def tile_deepseekv4attention_s_kernel(tc, query, key, value, attention_mask, sin
         work = ctx.enter_context(tc.tile_pool(name="work", bufs=4))
         small = ctx.enter_context(tc.tile_pool(name="small", bufs=4))
         results = ctx.enter_context(tc.tile_pool(name="results", bufs=4))
-        score_banks = ctx.enter_context(tc.psum_pool(name="score_banks", bufs=4))
+        score_banks = ctx.enter_context(tc.psum_pool(name="score_banks", bufs=5))
         flip_banks = ctx.enter_context(tc.psum_pool(name="flip_banks", bufs=3))
-        product_banks = ctx.enter_context(tc.psum_pool(name="product_banks", bufs=1))
 
         sinks_row = keep.tile([P, HEADS], BF16)
         ones_bf = keep.tile([P, P], BF16)
@@ -76,8 +75,8 @@ def tile_deepseekv4attention_s_kernel(tc, query, key, value, attention_mask, sin
         def load_mask(r):
             nc.sync.dma_start(out=mask_sb[r][:], in_=mask_dram[:, r, :])
 
-        load_k(0)
         load_q(0, 0, 1)
+        load_k(0)
         load_mask(0)
         load_mask(1)
         load_q(0, 1, Q_TILES)
@@ -104,25 +103,28 @@ def tile_deepseekv4attention_s_kernel(tc, query, key, value, attention_mask, sin
         v_codes = keep.tile([P, KV_HEADS, HEAD_DIM], U32, align_bytes=64)
         v_scales = keep.tile([P, KV_HEADS, HEAD_DIM], U8, align_bytes=64)
 
-        def flip(tiles):
-            flipped = flip_banks.tile([P, len(tiles), P], BF16, name="flipped", tag="flipped")
+        def flip(tiles, late=False):
+            if late:
+                flipped = score_banks.tile([P, len(tiles), P], BF16, name="flipped_late", tag="scores")
+            else:
+                flipped = flip_banks.tile([P, len(tiles), P], BF16, name="flipped", tag="flipped")
             for c, rows in enumerate(tiles):
                 nc.tensor.transpose(flipped[:, c, :], rows, identity_bf[:])
             return flipped
 
-        def flip_k(g):
-            return flip([k_sb[g][:, t, u, :] for u in range(HALVES) for t in range(K_TILES // HALVES)])
+        def flip_k(g, us=range(HALVES), late=False):
+            return flip([k_sb[g][:, t, u, :] for u in us for t in range(K_TILES // HALVES)], late)
 
-        def flip_q(g, rs):
-            return flip([q_sb[g, r][:, i, :] for r in rs for i in range(GROUP)])
+        def flip_q(g, rs, late=False):
+            return flip([q_sb[g, r][:, i, :] for r in rs for i in range(GROUP)], late)
 
-        def flip_mask(r):
+        def flip_mask(r, late=False):
             halfway = SEQ // HALVES
             return flip([
                 mask_sb[r][:, halfway * t + u : halfway * (t + 1) : HALVES]
                 for u in range(HALVES)
                 for t in range(K_TILES // HALVES)
-            ])
+            ], late)
 
         def keep_q(g, rs, flipped, copy):
             for k, r in enumerate(rs):
@@ -262,7 +264,7 @@ def tile_deepseekv4attention_s_kernel(tc, query, key, value, attention_mask, sin
             )
 
         def multiply_ev_pair(n):
-            product[n] = product_banks.tile([P, GROUP, HEAD_DIM], F32, name="product", tag="product")
+            product[n] = flip_banks.tile([P, GROUP, HEAD_DIM], F32, name="product", tag="flipped")
             for i in range(GROUP):
                 multiply_ev(GROUP * n + i, product[n][:, i, :])
 
@@ -305,39 +307,65 @@ def tile_deepseekv4attention_s_kernel(tc, query, key, value, attention_mask, sin
             nc.vector.tensor_scalar_mul(result[:], product[j][:], inv_den[n][:, i : i + 1])
             nc.sync.dma_start(out=out_dram[r, g][:, i, :], in_=result[:])
 
-        flipped_k = flip_k(0)
-        nc.vector.tensor_copy(out=kT[0][:], in_=flipped_k[:])
         flipped_q = flip_q(0, [0])
         keep_q(0, [0], flipped_q, nc.scalar.copy)
-        multiply_qk(0)
+        half = K_TILES // HALVES
+        for u, copy in enumerate((nc.vector.tensor_copy, nc.scalar.copy)):
+            flipped_k = flip_k(0, us=[u])
+            copy(out=kT[0][:, half * u : half * (u + 1), :], in_=flipped_k[:])
+        masked = work.tile([P, SEQ], F32, name="masked")
+        columns = SEQ // HALVES
+        half_banks = []
+        for u, (banks, tag) in enumerate(((score_banks, "scores"), (flip_banks, "flipped"))):
+            bank = banks.tile([P, columns], F32, name="half_scores", tag=tag)
+            nc.tensor.matmul(
+                out=bank[:],
+                lhsT=qT[0][0][:, 0, :],
+                rhs=kT[0][:, half * u : half * (u + 1), :].rearrange("d t p -> d (t p)"),
+                start=True,
+                stop=True,
+            )
+            half_banks.append(bank)
+        for u, bank in enumerate(half_banks):
+            nc.vector.scalar_tensor_tensor(
+                out=masked[:, columns * u : columns * (u + 1)],
+                in0=mask_sb[0][:, u : SEQ : HALVES],
+                scalar=INV_SCALING,
+                in1=bank[:],
+                op0=ALU.mult,
+                op1=ALU.add,
+            )
+        scores[0] = masked
         flipped_m = flip_mask(1)
         keep_mask(1, flipped_m)
         multiply_qk(1)
-        spread_sinks = product_banks.tile([P, HEADS], F32, name="spread_sinks", tag="product")
+        spread_sinks = flip_banks.tile([P, HEADS], F32, name="spread_sinks", tag="flipped")
         nc.tensor.matmul(out=spread_sinks[:], lhsT=ones_bf[:], rhs=sinks_row[:], start=True, stop=True)
         flipped_q = flip_q(0, [1])
         keep_q(0, [1], flipped_q, nc.scalar.copy)
-        flipped_m = flip_mask(2)
-        keep_mask(2, flipped_m)
+        flipped_m = flip_mask(2, late=True)
         multiply_qk(2)
-        add_mask(0)
-        group_value(0)
+        flipped_q = flip_q(0, [2, 3])
+        multiply_qk(3)
         row_max(0)
-        nc.vector.tensor_scalar_mul(neg_sinks[:], spread_sinks[:], -1.0)
         add_mask(1)
+        nc.vector.tensor_scalar_mul(neg_sinks[:], spread_sinks[:], -1.0)
         negative_max(0, 0, 1)
         row_max(1)
-        flipped_q = flip_q(0, [2, 3])
-        group_value(1)
+        keep_mask(2, flipped_m)
+        exponentials(0)
+        transpose_e(0)
+        keep_q(0, [2, 3], flipped_q, nc.scalar.copy)
+        group_value(0)
         negative_max(0, 1, GROUP)
 
         LAST = UNITS - GROUP
         for j in range(UNITS + 3):
             n, i = divmod(j, GROUP)
-            if 0 <= j - 1 < UNITS:
+            if 0 < j - 1 < UNITS:
                 transpose_e(j - 1)
-            if j + 3 < UNITS:
-                multiply_qk(j + 3)
+            if j + 4 < UNITS:
+                multiply_qk(j + 4)
             if i == 0 and 0 <= n - 2 < PAIRS - 1:
                 multiply_ev_pair(n - 2)
             if 0 <= j - 3 - LAST < GROUP:
@@ -345,36 +373,36 @@ def tile_deepseekv4attention_s_kernel(tc, query, key, value, attention_mask, sin
             if j in (LAST - 1, LAST, UNITS):
                 keep_warm()
             if j == 0:
-                flipped_m = flip_mask(3)
+                flipped_m = flip_mask(3, late=True)
             if j == 1:
                 flipped_k = flip_k(1)
-            if j == 3:
-                flipped_q = flip_q(1, [0, 1])
-            if j == 5:
-                flipped_q = flip_q(1, [2, 3])
+            if j == 2:
+                flipped_q = flip_q(1, [0, 1], late=True)
+            if j == 4:
+                flipped_q = flip_q(1, [2, 3], late=True)
             if j == 7:
-                flipped_m = flip_mask(0)
-            if j < UNITS:
+                flipped_m = flip_mask(0, late=True)
+            if 0 < j < UNITS:
                 exponentials(j)
-            if j == 0:
-                keep_q(0, [2, 3], flipped_q, nc.scalar.copy)
-            if j == 1:
-                keep_mask(3, flipped_m)
             if 0 <= j - 1 < UNITS:
                 group_e(j - 1)
             if i == 1 and n < PAIRS:
                 denominator(n)
+            if j == 1:
+                keep_mask(3, flipped_m)
             if j + 2 < UNITS:
                 row_max(j + 2)
             if j == 1:
+                group_value(1)
+            if j == 2:
                 quantise_value()
             if 0 <= j - 2 < UNITS:
                 quantise_e(j - 2)
             if j == 2:
                 nc.vector.tensor_copy(out=kT[1][:], in_=flipped_k[:])
-            if j == 4:
+            if j == 3:
                 keep_q(1, [0, 1], flipped_q, nc.vector.tensor_copy)
-            if j == 6:
+            if j == 5:
                 keep_q(1, [2, 3], flipped_q, nc.vector.tensor_copy)
             if j == 8:
                 keep_mask(0, flipped_m)

@@ -28,6 +28,7 @@ UNITS = PAIRS * GROUP
 SCALING = 1.0 / math.sqrt(HEAD_DIM)
 INV_SCALING = math.sqrt(HEAD_DIM)
 PAIR_ORDER = [(0, r) for r in range(Q_TILES)] + [(1, (r + 1) % Q_TILES) for r in range(Q_TILES)]
+VECTOR_GROUPS = (12, 13)
 VECTOR_PAIRS = 1
 
 FLOPS = 2 * 2 * HEADS * SEQ * SEQ * HEAD_DIM
@@ -238,9 +239,9 @@ def tile_deepseekv4attention_s_kernel(tc, query, key, value, attention_mask, sin
             for u in range(HALVES):
                 nc.tensor.transpose(e_flipped[j][:, u, :], e_words[:, u * P : (u + 1) * P], identity_f32[:])
 
-        def group_e(j):
+        def group_e(j, copy):
             e_grouped[j] = work.tile([P, P, HALVES], F32, name="e_grouped", align_bytes=64)
-            nc.scalar.copy(out=e_grouped[j][:], in_=e_flipped[j][:].rearrange("p u q -> p q u"))
+            copy(out=e_grouped[j][:], in_=e_flipped[j][:].rearrange("p u q -> p q u"))
 
         def quantise_e(j):
             e_codes[j] = work.tile([P, P], U32, name="e_codes", align_bytes=64)
@@ -364,6 +365,8 @@ def tile_deepseekv4attention_s_kernel(tc, query, key, value, attention_mask, sin
             n, i = divmod(j, GROUP)
             if 0 < j - 1 < UNITS:
                 transpose_e(j - 1)
+            if j == 0:
+                flipped_m = flip_mask(3, late=True)
             if j + 4 < UNITS:
                 multiply_qk(j + 4)
             if i == 0 and 0 <= n - 2 < PAIRS - 1:
@@ -372,8 +375,6 @@ def tile_deepseekv4attention_s_kernel(tc, query, key, value, attention_mask, sin
                 multiply_ev_unit(j - 3)
             if j in (LAST - 1, LAST, UNITS):
                 keep_warm()
-            if j == 0:
-                flipped_m = flip_mask(3, late=True)
             if j == 1:
                 flipped_k = flip_k(1)
             if j == 2:
@@ -384,8 +385,8 @@ def tile_deepseekv4attention_s_kernel(tc, query, key, value, attention_mask, sin
                 flipped_m = flip_mask(0, late=True)
             if 0 < j < UNITS:
                 exponentials(j)
-            if 0 <= j - 1 < UNITS:
-                group_e(j - 1)
+            if 0 <= j - 1 < UNITS and j - 1 not in VECTOR_GROUPS:
+                group_e(j - 1, nc.scalar.copy)
             if i == 1 and n < PAIRS:
                 denominator(n)
             if j == 1:
@@ -412,6 +413,8 @@ def tile_deepseekv4attention_s_kernel(tc, query, key, value, attention_mask, sin
                 invert_den(n - 2)
             if i == 1 and 0 <= n - 2 < PAIRS - 1:
                 divide_and_store(n - 2)
+            if j - 1 in VECTOR_GROUPS:
+                group_e(j - 1, nc.vector.tensor_copy)
             if j == LAST + 3:
                 invert_den(PAIRS - 1)
             if 0 <= j - 3 - LAST < GROUP:

@@ -56,6 +56,8 @@ def tile_deepseekv4attention_s_kernel(tc, query, key, value, attention_mask, sin
 
         sinks_row = keep.tile([P, HEADS], BF16)
         ones_bf = keep.tile([P, P], BF16)
+        zeros = keep.tile([P, P], F32)
+        nc.vector.memset(zeros[:], 0.0)
         nc.vector.memset(sinks_row[:], 0.0)
         nc.vector.memset(ones_bf[:], 1.0)
         nc.scalar.dma_start(out=sinks_row[0:1, :], in_=sinks.unsqueeze(0))
@@ -91,10 +93,8 @@ def tile_deepseekv4attention_s_kernel(tc, query, key, value, attention_mask, sin
         make_identity(nc, identity_bf[:])
         identity_f32 = keep.tile([P, P], F32)
         make_identity(nc, identity_f32[:])
-        zero = keep.tile([P, 1], F32)
         one = keep.tile([P, 1], F32)
-        nc.vector.memset(zero[:], 0.0)
-        nc.scalar.activation(out=one[:], in_=zero[:], func=ACT.Exp)
+        nc.scalar.activation(out=one[:], in_=zeros[:, 0:1], func=ACT.Exp)
         neg_sinks = keep.tile([P, HEADS], F32)
 
         kT = [keep.tile([P, K_TILES, P], BF16, name="kT%d" % g) for g in range(KV_HEADS)]
@@ -308,6 +308,13 @@ def tile_deepseekv4attention_s_kernel(tc, query, key, value, attention_mask, sin
             nc.vector.tensor_scalar_mul(result[:], product[j][:], inv_den[n][:, i : i + 1])
             nc.sync.dma_start(out=out_dram[r, g][:, i, :], in_=result[:])
 
+        warm_up = flip_banks.tile([P, P], F32, name="warm_up", tag="flipped")
+
+        def warm(times):
+            for k in range(times):
+                nc.tensor.matmul(out=warm_up[:], lhsT=zeros[:], rhs=zeros[:], start=True, stop=True)
+
+        warm(3)
         flipped_q = flip_q(0, [0])
         keep_q(0, [0], flipped_q, nc.scalar.copy)
         half = K_TILES // HALVES
@@ -337,21 +344,21 @@ def tile_deepseekv4attention_s_kernel(tc, query, key, value, attention_mask, sin
                 op1=ALU.add,
             )
         scores[0] = masked
+        spread_sinks = flip_banks.tile([P, HEADS], F32, name="spread_sinks", tag="flipped")
+        nc.tensor.matmul(out=spread_sinks[:], lhsT=ones_bf[:], rhs=sinks_row[:], start=True, stop=True)
         flipped_m = flip_mask(1)
         keep_mask(1, flipped_m)
         multiply_qk(1)
-        spread_sinks = flip_banks.tile([P, HEADS], F32, name="spread_sinks", tag="flipped")
-        nc.tensor.matmul(out=spread_sinks[:], lhsT=ones_bf[:], rhs=sinks_row[:], start=True, stop=True)
         flipped_q = flip_q(0, [1])
         keep_q(0, [1], flipped_q, nc.scalar.copy)
         flipped_m = flip_mask(2, late=True)
         multiply_qk(2)
         flipped_q = flip_q(0, [2, 3])
         multiply_qk(3)
-        row_max(0)
-        add_mask(1)
         nc.vector.tensor_scalar_mul(neg_sinks[:], spread_sinks[:], -1.0)
+        row_max(0)
         negative_max(0, 0, 1)
+        add_mask(1)
         row_max(1)
         keep_mask(2, flipped_m)
         exponentials(0)

import math
from contextlib import ExitStack

import concourse.mybir as mybir
from concourse.masks import make_identity

BF16 = mybir.dt.bfloat16
F32 = mybir.dt.float32
U32 = mybir.dt.uint32
U8 = mybir.dt.uint8
FP8X4 = mybir.dt.float8_e4m3fn_x4
ALU = mybir.AluOpType
ACT = mybir.ActivationFunctionType

P = 128
PACK = 4
PAIR = 2
HALVES = PACK // PAIR
HEADS = 4
KV_HEADS = 2
GROUP = HEADS // KV_HEADS
SEQ = 512
HEAD_DIM = 128
Q_TILES = SEQ // P
K_TILES = SEQ // P
PAIRS = KV_HEADS * Q_TILES
UNITS = PAIRS * GROUP
SCALING = 1.0 / math.sqrt(HEAD_DIM)
INV_SCALING = math.sqrt(HEAD_DIM)
PAIR_ORDER = [(0, r) for r in range(Q_TILES)] + [(1, (r + 1) % Q_TILES) for r in range(Q_TILES)]
VECTOR_GROUPS = (12, 13)
VECTOR_PAIRS = 1

FLOPS = 2 * 2 * HEADS * SEQ * SEQ * HEAD_DIM


def tile_deepseekv4attention_s_kernel(tc, query, key, value, attention_mask, sinks, out):
    nc = tc.nc

    q_dram = [
        query[0, GROUP * g : GROUP * (g + 1)].rearrange("i (p r) d -> p i r d", r=Q_TILES) for g in range(KV_HEADS)
    ]
    mask_dram = attention_mask[0, 0].rearrange("(p r) k -> p r k", r=Q_TILES)
    out_dram = out[0].rearrange("(p r) (g i) d -> r g p i d", r=Q_TILES, i=GROUP)
    k_dram = [key[0, g].rearrange("(t p u) d -> p t (u d)", p=P, u=HALVES) for g in range(KV_HEADS)]
    v_dram = value[0].rearrange("g (p t) d -> p g (t d)", t=PACK)

    with ExitStack() as ctx:
        ctx.enter_context(tc.manual_schedule())
        keep = ctx.enter_context(tc.tile_pool(name="keep", bufs=1))
        work = ctx.enter_context(tc.tile_pool(name="work", bufs=4))
        small = ctx.enter_context(tc.tile_pool(name="small", bufs=4))
        results = ctx.enter_context(tc.tile_pool(name="results", bufs=4))
        score_banks = ctx.enter_context(tc.psum_pool(name="score_banks", bufs=5))
        flip_banks = ctx.enter_context(tc.psum_pool(name="flip_banks", bufs=3))

        sinks_row = keep.tile([P, HEADS], BF16)
        ones_bf = keep.tile([P, P], BF16)
        zeros = keep.tile([P, P], F32)
        nc.vector.memset(zeros[:], 0.0)
        nc.vector.memset(sinks_row[:], 0.0)
        nc.vector.memset(ones_bf[:], 1.0)
        nc.scalar.dma_start(out=sinks_row[0:1, :], in_=sinks.unsqueeze(0))
        k_sb = [keep.tile([P, K_TILES // HALVES, HALVES, HEAD_DIM], BF16, name="k_sb%d" % g) for g in range(KV_HEADS)]
        q_sb = {}
        mask_sb = [keep.tile([P, SEQ], BF16, name="mask_sb%d" % r) for r in range(Q_TILES)]
        v_sb = keep.tile([P, KV_HEADS, PACK, HEAD_DIM], BF16)

        def load_k(g):
            nc.sync.dma_start(out=k_sb[g][:].rearrange("p t u d -> p t (u d)"), in_=k_dram[g])

        def load_q(g, first, last):
            rows = keep.tile([P, GROUP, last - first, HEAD_DIM], BF16, name="q_sb%d_%d" % (g, first))
            nc.sync.dma_start(out=rows[:], in_=q_dram[g][:, :, first:last, :])
            for r in range(first, last):
                q_sb[g, r] = rows[:, :, r - first, :]

        def load_mask(r):
            nc.sync.dma_start(out=mask_sb[r][:], in_=mask_dram[:, r, :])

        load_q(0, 0, 1)
        load_k(0)
        load_mask(0)
        load_mask(1)
        load_q(0, 1, Q_TILES)
        load_mask(2)
        nc.sync.dma_start(out=v_sb[:].rearrange("p g t d -> p g (t d)"), in_=v_dram)
        load_mask(3)
        load_k(1)
        load_q(1, 0, Q_TILES)

        identity_bf = keep.tile([P, P], BF16)
        make_identity(nc, identity_bf[:])
        identity_f32 = keep.tile([P, P], F32)
        make_identity(nc, identity_f32[:])
        one = keep.tile([P, 1], F32)
        nc.scalar.activation(out=one[:], in_=zeros[:, 0:1], func=ACT.Exp)
        neg_sinks = keep.tile([P, HEADS], F32)

        kT = [keep.tile([P, K_TILES, P], BF16, name="kT%d" % g) for g in range(KV_HEADS)]
        qT = [[keep.tile([P, GROUP, P], BF16, name="qT%d_%d" % (g, r)) for r in range(Q_TILES)] for g in range(KV_HEADS)]
        maskT = [keep.tile([P, K_TILES, P], F32, name="maskT%d" % r) for r in range(Q_TILES)]
        v_grouped = keep.tile([P, KV_HEADS, HEAD_DIM, PACK], BF16, align_bytes=64)
        v_codes = keep.tile([P, KV_HEADS, HEAD_DIM], U32, align_bytes=64)
        v_scales = keep.tile([P, KV_HEADS, HEAD_DIM], U8, align_bytes=64)

        def flip(tiles, late=False):
            if late:
                flipped = score_banks.tile([P, len(tiles), P], BF16, name="flipped_late", tag="scores")
            else:
                flipped = flip_banks.tile([P, len(tiles), P], BF16, name="flipped", tag="flipped")
            for c, rows in enumerate(tiles):
                nc.tensor.transpose(flipped[:, c, :], rows, identity_bf[:])
            return flipped

        def flip_k(g, us=range(HALVES), late=False):
            return flip([k_sb[g][:, t, u, :] for u in us for t in range(K_TILES // HALVES)], late)

        def flip_q(g, rs, late=False):
            return flip([q_sb[g, r][:, i, :] for r in rs for i in range(GROUP)], late)

        def flip_mask(r, late=False):
            halfway = SEQ // HALVES
            return flip([
                mask_sb[r][:, halfway * t + u : halfway * (t + 1) : HALVES]
                for u in range(HALVES)
                for t in range(K_TILES // HALVES)
            ], late)

        def keep_q(g, rs, flipped, copy):
            for k, r in enumerate(rs):
                copy(out=qT[g][r][:], in_=flipped[:, GROUP * k : GROUP * (k + 1), :])

        def keep_mask(r, flipped):
            nc.scalar.activation(out=maskT[r][:], in_=flipped[:], func=ACT.Copy, scale=INV_SCALING)

        def group_value(g):
            nc.vector.tensor_copy(
                out=v_grouped[:, g].rearrange("p d (u e) -> p d u e", u=HALVES),
                in_=v_sb[:, g].rearrange("p (e u) d -> p d u e", u=HALVES),
            )

        def quantise_value():
            nc.vector.quantize_mx(
                out=v_codes[:].rearrange("p g d -> p (g d)").bitcast(FP8X4),
                scales=v_scales[:].rearrange("p g d -> p (g d)"),
                in_=v_grouped[:].rearrange("p g d t -> p (g d t)"),
            )

        scores, e_bf, e_flipped, e_grouped, e_codes, e_scales = ({}, {}, {}, {}, {}, {})
        neg_x, neg_max, row_sum, sink_arg, sink_e, den, inv_den, product = ({}, {}, {}, {}, {}, {}, {}, {})

        def multiply_qk(j):
            n, i = divmod(j, GROUP)
            g, r = PAIR_ORDER[n]
            scores[j] = score_banks.tile([P, SEQ], F32, name="scores", tag="scores")
            on_tensor = n >= VECTOR_PAIRS
            if on_tensor:
                for c in range(K_TILES):
                    nc.tensor.matmul(
                        out=scores[j][:, c * P : (c + 1) * P],
                        lhsT=maskT[r][:, c, :],
                        rhs=identity_f32[:],
                        start=(c == 0),
                        stop=False,
                        is_transpose=True,
                    )
            nc.tensor.matmul(
                out=scores[j][:],
                lhsT=qT[g][r][:, i, :],
                rhs=kT[g][:].rearrange("d t p -> d (t p)"),
                start=not on_tensor,
                stop=True,
            )

        def add_mask(j):
            n = j // GROUP
            if n >= VECTOR_PAIRS:
                return
            r = PAIR_ORDER[n][1]
            masked = work.tile([P, SEQ], F32, name="masked")
            nc.vector.scalar_tensor_tensor(
                out=masked[:].rearrange("p (u j) -> p u j", u=HALVES),
                in0=mask_sb[r][:].rearrange("p (j u) -> p u j", u=HALVES),
                scalar=INV_SCALING,
                in1=scores[j][:].rearrange("p (u j) -> p u j", u=HALVES),
                op0=ALU.mult,
                op1=ALU.add,
            )
            scores[j] = masked

        def row_max(j):
            n, i = divmod(j, GROUP)
            if i == 0:
                neg_x[n] = small.tile([P, GROUP], F32, name="neg_x")
            nc.vector.tensor_reduce(
                out=neg_x[n][:, i : i + 1], in_=scores[j][:], axis=mybir.AxisListType.X, op=ALU.max, negate=True
            )

        def negative_max(n, first=0, last=GROUP):
            g = PAIR_ORDER[n][0]
            if first == 0:
                neg_max[n] = small.tile([P, GROUP], F32, name="neg_max")
            nc.vector.scalar_tensor_tensor(
                out=neg_max[n][:, first:last],
                in0=neg_x[n][:, first:last],
                scalar=SCALING,
                in1=neg_sinks[:, GROUP * g + first : GROUP * g + last],
                op0=ALU.mult,
                op1=ALU.min,
            )
            if last == GROUP:
                sink_arg[n] = small.tile([P, GROUP], F32, name="sink_arg")
                nc.gpsimd.tensor_sub(sink_arg[n][:], neg_max[n][:], neg_sinks[:, GROUP * g : GROUP * (g + 1)])

        def exponentials(j):
            n, i = divmod(j, GROUP)
            if i == 0:
                row_sum[n] = small.tile([P, GROUP], F32, name="row_sum")
            e_bf[j] = work.tile([P, SEQ], BF16, name="e_bf")
            nc.scalar.activation(
                out=e_bf[j][:],
                in_=scores[j][:],
                func=ACT.Exp,
                bias=neg_max[n][:, i : i + 1],
                scale=SCALING,
                accum_out=row_sum[n][:, i : i + 1],
            )

        def denominator(n):
            sink_e[n] = small.tile([P, GROUP], F32, name="sink_e")
            nc.scalar.activation(out=sink_e[n][:], in_=sink_arg[n][:], func=ACT.Exp)
            den[n] = small.tile([P, GROUP], F32, name="den")
            nc.gpsimd.tensor_add(den[n][:], row_sum[n][:], sink_e[n][:])

        def transpose_e(j):
            e_words = e_bf[j][:].bitcast(F32)
            e_flipped[j] = flip_banks.tile([P, HALVES, P], F32, name="e_flipped", tag="flipped")
            for u in range(HALVES):
                nc.tensor.transpose(e_flipped[j][:, u, :], e_words[:, u * P : (u + 1) * P], identity_f32[:])

        def group_e(j, copy):
            e_grouped[j] = work.tile([P, P, HALVES], F32, name="e_grouped", align_bytes=64)
            copy(out=e_grouped[j][:], in_=e_flipped[j][:].rearrange("p u q -> p q u"))

        def quantise_e(j):
            e_codes[j] = work.tile([P, P], U32, name="e_codes", align_bytes=64)
            e_scales[j] = work.tile([P, P], U8, name="e_scales", align_bytes=64)
            nc.vector.quantize_mx(
                out=e_codes[j][:].bitcast(FP8X4),
                scales=e_scales[j][:],
                in_=e_grouped[j][:].rearrange("p q u -> p (q u)").bitcast(BF16),
            )

        def multiply_ev(j, out):
            g = PAIR_ORDER[j // GROUP][0]
            nc.tensor.matmul_mx(
                out=out,
                lhsT=e_codes[j][:].bitcast(FP8X4),
                lhsT_scale=e_scales[j][:],
                rhs=v_codes[:, g, :].bitcast(FP8X4),
                rhs_scale=v_scales[:, g, :],
                start=True,
                stop=True,
            )

        def multiply_ev_pair(n):
            product[n] = flip_banks.tile([P, GROUP, HEAD_DIM], F32, name="product", tag="flipped")
            for i in range(GROUP):
                multiply_ev(GROUP * n + i, product[n][:, i, :])

        def multiply_ev_unit(j):
            product[j] = score_banks.tile([P, HEAD_DIM], F32, name="product_unit", tag="scores")
            multiply_ev(j, product[j][:])

        def keep_warm():
            idle = score_banks.tile([P, KV_HEADS * HEAD_DIM], F32, name="idle", tag="scores")
            for k in range(2):
                nc.tensor.matmul_mx(
                    out=idle[:],
                    lhsT=v_codes[:, 0, :].bitcast(FP8X4),
                    lhsT_scale=v_scales[:, 0, :],
                    rhs=v_codes[:].rearrange("p g d -> p (g d)").bitcast(FP8X4),
                    rhs_scale=v_scales[:].rearrange("p g d -> p (g d)"),
                    start=True,
                    stop=True,
                )

        def invert_den(n):
            inv_den[n] = small.tile([P, GROUP], F32, name="inv_den")
            nc.vector.reciprocal(out=inv_den[n][:], in_=den[n][:])

        def divide_and_store(n):
            g, r = PAIR_ORDER[n]
            result = results.tile([P, GROUP, HEAD_DIM], F32)
            nc.vector.tensor_tensor(
                out=result[:],
                in0=product[n][:],
                in1=inv_den[n][:].unsqueeze(2).to_broadcast([P, GROUP, HEAD_DIM]),
                op=ALU.mult,
            )
            nc.sync.dma_start(out=out_dram[r, g], in_=result[:])

        def divide_and_store_unit(j):
            n, i = divmod(j, GROUP)
            g, r = PAIR_ORDER[n]
            result = results.tile([P, HEAD_DIM], F32, name="result_unit")
            nc.vector.tensor_scalar_mul(result[:], product[j][:], inv_den[n][:, i : i + 1])
            nc.sync.dma_start(out=out_dram[r, g][:, i, :], in_=result[:])

        warm_up = flip_banks.tile([P, P], F32, name="warm_up", tag="flipped")

        def warm(times):
            for k in range(times):
                nc.tensor.matmul(out=warm_up[:], lhsT=zeros[:], rhs=zeros[:], start=True, stop=True)

        warm(3)
        flipped_q = flip_q(0, [0])
        keep_q(0, [0], flipped_q, nc.scalar.copy)
        half = K_TILES // HALVES
        for u, copy in enumerate((nc.vector.tensor_copy, nc.scalar.copy)):
            flipped_k = flip_k(0, us=[u])
            copy(out=kT[0][:, half * u : half * (u + 1), :], in_=flipped_k[:])
        masked = work.tile([P, SEQ], F32, name="masked")
        columns = SEQ // HALVES
        half_banks = []
        for u, (banks, tag) in enumerate(((score_banks, "scores"), (flip_banks, "flipped"))):
            bank = banks.tile([P, columns], F32, name="half_scores", tag=tag)
            nc.tensor.matmul(
                out=bank[:],
                lhsT=qT[0][0][:, 0, :],
                rhs=kT[0][:, half * u : half * (u + 1), :].rearrange("d t p -> d (t p)"),
                start=True,
                stop=True,
            )
            half_banks.append(bank)
        for u, bank in enumerate(half_banks):
            nc.vector.scalar_tensor_tensor(
                out=masked[:, columns * u : columns * (u + 1)],
                in0=mask_sb[0][:, u : SEQ : HALVES],
                scalar=INV_SCALING,
                in1=bank[:],
                op0=ALU.mult,
                op1=ALU.add,
            )
        scores[0] = masked
        spread_sinks = flip_banks.tile([P, HEADS], F32, name="spread_sinks", tag="flipped")
        nc.tensor.matmul(out=spread_sinks[:], lhsT=ones_bf[:], rhs=sinks_row[:], start=True, stop=True)
        flipped_m = flip_mask(1)
        keep_mask(1, flipped_m)
        multiply_qk(1)
        flipped_q = flip_q(0, [1])
        keep_q(0, [1], flipped_q, nc.scalar.copy)
        flipped_m = flip_mask(2, late=True)
        multiply_qk(2)
        flipped_q = flip_q(0, [2, 3])
        multiply_qk(3)
        nc.vector.tensor_scalar_mul(neg_sinks[:], spread_sinks[:], -1.0)
        row_max(0)
        negative_max(0, 0, 1)
        add_mask(1)
        row_max(1)
        keep_mask(2, flipped_m)
        exponentials(0)
        transpose_e(0)
        keep_q(0, [2, 3], flipped_q, nc.scalar.copy)
        group_value(0)
        negative_max(0, 1, GROUP)

        LAST = UNITS - GROUP
        for j in range(UNITS + 3):
            n, i = divmod(j, GROUP)
            if 0 < j - 1 < UNITS:
                transpose_e(j - 1)
            if j == 0:
                flipped_m = flip_mask(3, late=True)
            if j + 4 < UNITS:
                multiply_qk(j + 4)
            if i == 0 and 0 <= n - 2 < PAIRS - 1:
                multiply_ev_pair(n - 2)
            if 0 <= j - 3 - LAST < GROUP:
                multiply_ev_unit(j - 3)
            if j in (LAST - 1, LAST, UNITS):
                keep_warm()
            if j == 1:
                flipped_k = flip_k(1)
            if j == 2:
                flipped_q = flip_q(1, [0, 1], late=True)
            if j == 4:
                flipped_q = flip_q(1, [2, 3], late=True)
            if j == 7:
                flipped_m = flip_mask(0, late=True)
            if 0 < j < UNITS:
                exponentials(j)
            if 0 <= j - 1 < UNITS and j - 1 not in VECTOR_GROUPS:
                group_e(j - 1, nc.scalar.copy)
            if i == 1 and n < PAIRS:
                denominator(n)
            if j == 1:
                keep_mask(3, flipped_m)
            if j + 2 < UNITS:
                row_max(j + 2)
            if j == 1:
                group_value(1)
            if j == 2:
                quantise_value()
            if 0 <= j - 2 < UNITS:
                quantise_e(j - 2)
            if j == 2:
                nc.vector.tensor_copy(out=kT[1][:], in_=flipped_k[:])
            if j == 3:
                keep_q(1, [0, 1], flipped_q, nc.vector.tensor_copy)
            if j == 5:
                keep_q(1, [2, 3], flipped_q, nc.vector.tensor_copy)
            if j == 8:
                keep_mask(0, flipped_m)
            if i == 1 and n + 1 < PAIRS:
                negative_max(n + 1)
            if i == 0 and 0 <= n - 2 < PAIRS - 1:
                invert_den(n - 2)
            if i == 1 and 0 <= n - 2 < PAIRS - 1:
                divide_and_store(n - 2)
            if j - 1 in VECTOR_GROUPS:
                group_e(j - 1, nc.vector.tensor_copy)
            if j == LAST + 3:
                invert_den(PAIRS - 1)
            if 0 <= j - 3 - LAST < GROUP:
                divide_and_store_unit(j - 3)
